import numpy as np
import ml_dtypes

BF16 = ml_dtypes.bfloat16


def bf(x):
    return np.asarray(x, np.float32).astype(BF16)


def f32(x):
    return np.asarray(x, np.float32)


def f64(x):
    return np.asarray(x).astype(np.float64)


def striped(idx):
    return np.tile(idx.reshape(-1, 16).T, (8, 1))


D, S, N, E, H, D2, EO, R, DO, B, NE = 128, 4096, 1024, 512, 512, 512, 1024, 256, 256, 8, 64


def relu(v):
    return np.maximum(v, 0.0)


def setup_inputs():
    rn = np.random.standard_normal
    return {
        "table": bf(rn((D, S))),
        "ws1": bf(rn((D, H)) / np.sqrt(D)), "bs1": f32(0.1 * rn((H, 1))),
        "ws2": bf(rn((H, D2)) * np.sqrt(2.0 / H)), "bs2": f32(0.1 * rn((D2, 1))),
        "we1": bf(rn((D, H)) / np.sqrt(D)), "be1": f32(0.1 * rn((H, 1))),
        "we2": bf(rn((H, D2)) * np.sqrt(2.0 / H)), "be2": f32(0.1 * rn((D2, 1))),
        "wo": bf(rn((D2 + D2, EO)) * np.sqrt(2.0 / (D2 + D2))), "bo": f32(0.1 * rn((EO, 1))),
        "wr1": bf(rn((EO + EO, R)) / np.sqrt(EO + EO)), "br1": f32(0.1 * rn((R, 1))),
        "wr2": bf(rn((R, DO)) * np.sqrt(2.0 / R)), "br2": f32(0.1 * rn((DO, 1))),
        "offs": striped(np.random.permutation(np.tile(np.arange(S), 2))[:N]),
    }


def reference(table, ws1, bs1, ws2, bs2, we1, be1, we2, be2, wo, bo, wr1, br1, wr2, br2, offs):
    idx = offs[:16].T.reshape(-1)
    picked = f64(table)[:, idx]
    a_s = relu(f64(ws1).T @ picked[:, :E] + f64(bs1))
    a_e = relu(f64(we1).T @ picked[:, E:] + f64(be1))
    r_s = f64(ws2).T @ a_s + f64(bs2)
    r_e = f64(we2).T @ a_e + f64(be2)
    cat = relu(np.concatenate([r_s, r_e], axis=0))
    ent = f64(wo).T @ cat + f64(bo)
    hp = f64(wr1)[:EO].T @ ent
    hq = f64(wr1)[EO:].T @ ent
    hid = relu(hp.reshape(R, B, NE, 1) + hq.reshape(R, B, 1, NE) + f64(br1).reshape(R, 1, 1, 1))
    return f64(wr2).T @ hid.reshape(R, B * NE * NE) + f64(br2)

@@ -1,0 +1,158 @@
+import concourse.mybir as mybir
+from concourse.masks import make_identity
+
+BF16 = mybir.dt.bfloat16
+F32 = mybir.dt.float32
+U16 = mybir.dt.uint16
+ADD = mybir.AluOpType.add
+MAX = mybir.AluOpType.max
+RELU = mybir.ActivationFunctionType.Relu
+IDENTITY = mybir.ActivationFunctionType.Identity
+
+P = 128
+S = 4096
+E = 512
+H = 512
+EO = 1024
+R = 256
+DO = 256
+B = 8
+NE = 64
+FIRSTS = E // NE
+STORE = 2048
+
+FLOPS = 2 * (P * H * 2 * E + 2 * H * H * E + EO * EO * E + 2 * EO * R * E + R * DO * B * NE * NE)
+
+
+def add_bias(nc, turn, dest, acc, bias_col, relu):
+    if turn % 2 == 0:
+        nc.scalar.activation(dest, acc, RELU if relu else IDENTITY, bias=bias_col)
+    elif relu:
+        nc.vector.tensor_scalar(dest, acc, bias_col, 0.0, ADD, MAX)
+    else:
+        nc.vector.tensor_scalar_add(dest, acc, bias_col)
+
+
+def project(nc, psum, weights, first_k, moving, m):
+    acc = psum.tile([P, E], F32, name="acc")
+    last = len(moving) - 1
+    for k, block in enumerate(moving):
+        nc.tensor.matmul(
+            acc[:], weights[:, first_k + k, m * P : (m + 1) * P], block[:], start=(k == 0), stop=(k == last)
+        )
+    return acc
+
+
+def tile_efficientrelationshipmodel_b_kernel(
+    tc, table, ws1, bs1, ws2, bs2, we1, be1, we2, be2, wo, bo, wr1, br1, wr2, br2, offs, out
+):
+    nc = tc.nc
+    with (
+        tc.tile_pool(name="held", bufs=1) as held,
+        tc.tile_pool(name="pairs", bufs=4) as pairs,
+        tc.tile_pool(name="staging", bufs=3) as staging,
+        tc.psum_pool(name="psum", bufs=8) as psum,
+    ):
+        offsets = held.tile([P, 2 * E // 16], U16, name="offsets")
+        nc.sync.dma_start(offsets[:], offs)
+        table_sb = held.tile([P, S], BF16, name="table_sb")
+        nc.sync.dma_start(table_sb[:], table)
+
+        def load_blocks(queue, name, weights):
+            rows, columns = weights.shape
+            tile = held.tile([P, rows // P, columns], BF16, name=name)
+            queue.dma_start(tile[:], weights.rearrange("(k p) c -> p k c", p=P))
+            return tile
+
+        ws1_sb = load_blocks(nc.scalar, "ws1_sb", ws1)
+        we1_sb = load_blocks(nc.scalar, "we1_sb", we1)
+        ws2_sb = load_blocks(nc.scalar, "ws2_sb", ws2)
+        we2_sb = load_blocks(nc.scalar, "we2_sb", we2)
+        wo_sb = load_blocks(nc.sync, "wo_sb", wo)
+        wr1_sb = load_blocks(nc.scalar, "wr1_sb", wr1)
+        wr2_sb = load_blocks(nc.scalar, "wr2_sb", wr2)
+
+        bias_rows = held.tile([P, P], F32, name="bias_rows")
+        nc.vector.memset(bias_rows[:], 0.0)
+        first_col = {}
+        rows_used = 0
+        for name, vector in (
+            ("bs1", bs1), ("be1", be1), ("bs2", bs2), ("be2", be2), ("bo", bo), ("br1", br1), ("br2", br2)
+        ):
+            blocks = vector.shape[0] // P
+            nc.gpsimd.dma_start(
+                bias_rows[rows_used : rows_used + blocks, :], vector.rearrange("(k p) o -> k (p o)", p=P)
+            )
+            first_col[name] = rows_used
+            rows_used += blocks
+        identity = held.tile([P, P], F32, name="identity")
+        make_identity(nc, identity[:])
+        flipped = psum.tile([P, E], F32, name="acc")
+        nc.tensor.transpose(flipped[:, 0:P], bias_rows[:], identity[:])
+        bias_cols = held.tile([P, P], F32, name="bias_cols")
+        nc.vector.tensor_copy(bias_cols[:], flipped[:, 0:P])
+
+        def bias(name, block):
+            col = first_col[name] + block
+            return bias_cols[:, col : col + 1]
+
+        a = []
+        for half, (w1_sb, b1) in enumerate(((ws1_sb, "bs1"), (we1_sb, "be1"))):
+            picked = table_sb[:].indirect(offsets[:, half * (E // 16) : (half + 1) * (E // 16)])
+            a.append([])
+            for m in range(H // P):
+                acc = psum.tile([P, E], F32, name="acc")
+                nc.tensor.matmul(acc[:], w1_sb[:, 0, m * P : (m + 1) * P], picked, start=True, stop=True)
+                a_block = held.tile([P, E], BF16, name=f"a{half}_{m}")
+                add_bias(nc, m, a_block[:], acc[:], bias(b1, m), relu=True)
+                a[half].append(a_block)
+
+        cat = []
+        for half, (w2_sb, b2) in enumerate(((ws2_sb, "bs2"), (we2_sb, "be2"))):
+            for m in range(H // P):
+                acc = project(nc, psum, w2_sb, 0, a[half], m)
+                cat_block = held.tile([P, E], BF16, name=f"cat{half}_{m}")
+                add_bias(nc, m, cat_block[:], acc[:], bias(b2, m), relu=True)
+                cat.append(cat_block)
+
+        ent = []
+        for m in range(EO // P):
+            acc = project(nc, psum, wo_sb, 0, cat, m)
+            ent_block = held.tile([P, E], BF16, name=f"ent{m}")
+            add_bias(nc, m, ent_block[:], acc[:], bias("bo", m), relu=False)
+            ent.append(ent_block)
+
+        hp = []
+        hq = []
+        for m in range(R // P):
+            acc = project(nc, psum, wr1_sb, 0, ent, m)
+            hp_block = held.tile([P, E], F32, name=f"hp{m}")
+            nc.scalar.activation(hp_block[:], acc[:], IDENTITY, bias=bias("br1", m))
+            hp.append(hp_block)
+            acc = project(nc, psum, wr1_sb, EO // P, ent, m)
+            hq_block = held.tile([P, E], F32, name=f"hq{m}")
+            nc.vector.tensor_copy(hq_block[:], acc[:])
+            hq.append(hq_block)
+
+        for u in range(B):
+            seconds = slice(u * NE, (u + 1) * NE)
+            for group in range(NE // FIRSTS):
+                column = (u * NE + group * FIRSTS) * NE
+                hid = []
+                for m in range(R // P):
+                    hid_block = pairs.tile([P, E], BF16, name=f"hid{m}")
+                    for i in range(FIRSTS):
+                        p = u * NE + group * FIRSTS + i
+                        nc.vector.tensor_scalar(
+                            hid_block[:, i * NE : (i + 1) * NE], hq[m][:, seconds], hp[m][:, p : p + 1], 0.0, ADD, MAX
+                        )
+                    hid.append(hid_block)
+                if column % STORE == 0:
+                    staged = [staging.tile([P, STORE], F32, name=f"staged{d}") for d in range(DO // P)]
+                for d in range(DO // P):
+                    acc = project(nc, psum, wr2_sb, 0, hid, d)
+                    at = column % STORE
+                    nc.scalar.activation(staged[d][:, at : at + E], acc[:], IDENTITY, bias=bias("br2", d))
+                if (column + E) % STORE == 0:
+                    for d in range(DO // P):
+                        nc.sync.dma_start(out[d * P : (d + 1) * P, column + E - STORE : column + E], staged[d][:])

@@ -66,11 +66,6 @@ def tile_efficientrelationshipmodel_b_kernel(
 
         ws1_sb = load_blocks(nc.scalar, "ws1_sb", ws1)
         we1_sb = load_blocks(nc.scalar, "we1_sb", we1)
-        ws2_sb = load_blocks(nc.scalar, "ws2_sb", ws2)
-        we2_sb = load_blocks(nc.scalar, "we2_sb", we2)
-        wo_sb = load_blocks(nc.sync, "wo_sb", wo)
-        wr1_sb = load_blocks(nc.scalar, "wr1_sb", wr1)
-        wr2_sb = load_blocks(nc.scalar, "wr2_sb", wr2)
 
         bias_rows = held.tile([P, P], F32, name="bias_rows")
         nc.vector.memset(bias_rows[:], 0.0)
@@ -80,11 +75,18 @@ def tile_efficientrelationshipmodel_b_kernel(
             ("bs1", bs1), ("be1", be1), ("bs2", bs2), ("be2", be2), ("bo", bo), ("br1", br1), ("br2", br2)
         ):
             blocks = vector.shape[0] // P
-            nc.gpsimd.dma_start(
+            nc.scalar.dma_start(
                 bias_rows[rows_used : rows_used + blocks, :], vector.rearrange("(k p) o -> k (p o)", p=P)
             )
             first_col[name] = rows_used
             rows_used += blocks
+
+        ws2_sb = load_blocks(nc.sync, "ws2_sb", ws2)
+        we2_sb = load_blocks(nc.sync, "we2_sb", we2)
+        wo_sb = load_blocks(nc.sync, "wo_sb", wo)
+        wr1_sb = load_blocks(nc.sync, "wr1_sb", wr1)
+        wr2_sb = load_blocks(nc.sync, "wr2_sb", wr2)
+
         identity = held.tile([P, P], F32, name="identity")
         make_identity(nc, identity[:])
         flipped = psum.tile([P, E], F32, name="acc")
@@ -149,10 +151,14 @@ def tile_efficientrelationshipmodel_b_kernel(
                     hid.append(hid_block)
                 if column % STORE == 0:
                     staged = [staging.tile([P, STORE], F32, name=f"staged{d}") for d in range(DO // P)]
+                at = column % STORE
                 for d in range(DO // P):
                     acc = project(nc, psum, wr2_sb, 0, hid, d)
-                    at = column % STORE
                     nc.scalar.activation(staged[d][:, at : at + E], acc[:], IDENTITY, bias=bias("br2", d))
-                if (column + E) % STORE == 0:
+                width = E if column >= B * NE * NE - STORE else STORE
+                if (column + E) % width == 0:
                     for d in range(DO // P):
-                        nc.sync.dma_start(out[d * P : (d + 1) * P, column + E - STORE : column + E], staged[d][:])
+                        nc.sync.dma_start(
+                            out[d * P : (d + 1) * P, column + E - width : column + E],
+                            staged[d][:, at + E - width : at + E],
+                        )

@@ -55,37 +55,36 @@ def tile_efficientrelationshipmodel_b_kernel(
     ):
         offsets = held.tile([P, 2 * E // 16], U16, name="offsets")
         nc.sync.dma_start(offsets[:], offs)
-        table_sb = held.tile([P, S], BF16, name="table_sb")
-        nc.sync.dma_start(table_sb[:], table)
-
-        def load_blocks(queue, name, weights):
-            rows, columns = weights.shape
-            tile = held.tile([P, rows // P, columns], BF16, name=name)
-            queue.dma_start(tile[:], weights.rearrange("(k p) c -> p k c", p=P))
-            return tile
-
-        ws1_sb = load_blocks(nc.scalar, "ws1_sb", ws1)
-        we1_sb = load_blocks(nc.scalar, "we1_sb", we1)
 
         bias_rows = held.tile([P, P], F32, name="bias_rows")
-        nc.vector.memset(bias_rows[:], 0.0)
+        nc.gpsimd.memset(bias_rows[:], 0.0)
         first_col = {}
         rows_used = 0
         for name, vector in (
             ("bs1", bs1), ("be1", be1), ("bs2", bs2), ("be2", be2), ("bo", bo), ("br1", br1), ("br2", br2)
         ):
             blocks = vector.shape[0] // P
-            nc.scalar.dma_start(
+            nc.sync.dma_start(
                 bias_rows[rows_used : rows_used + blocks, :], vector.rearrange("(k p) o -> k (p o)", p=P)
             )
             first_col[name] = rows_used
             rows_used += blocks
 
-        ws2_sb = load_blocks(nc.sync, "ws2_sb", ws2)
-        we2_sb = load_blocks(nc.sync, "we2_sb", we2)
-        wo_sb = load_blocks(nc.sync, "wo_sb", wo)
-        wr1_sb = load_blocks(nc.sync, "wr1_sb", wr1)
-        wr2_sb = load_blocks(nc.sync, "wr2_sb", wr2)
+        def load_blocks(name, weights):
+            rows, columns = weights.shape
+            tile = held.tile([P, rows // P, columns], BF16, name=name)
+            nc.sync.dma_start(tile[:], weights.rearrange("(k p) c -> p k c", p=P))
+            return tile
+
+        ws1_sb = load_blocks("ws1_sb", ws1)
+        table_sb = held.tile([P, S], BF16, name="table_sb")
+        nc.sync.dma_start(table_sb[:], table)
+        we1_sb = load_blocks("we1_sb", we1)
+        ws2_sb = load_blocks("ws2_sb", ws2)
+        we2_sb = load_blocks("we2_sb", we2)
+        wo_sb = load_blocks("wo_sb", wo)
+        wr1_sb = load_blocks("wr1_sb", wr1)
+        wr2_sb = load_blocks("wr2_sb", wr2)
 
         identity = held.tile([P, P], F32, name="identity")
         make_identity(nc, identity[:])

@@ -20,12 +20,13 @@ B = 8
 NE = 64
 FIRSTS = E // NE
 STORE = 2048
+VECTOR_DRAINS = 8
 
 FLOPS = 2 * (P * H * 2 * E + 2 * H * H * E + EO * EO * E + 2 * EO * R * E + R * DO * B * NE * NE)
 
 
-def add_bias(nc, turn, dest, acc, bias_col, relu):
-    if turn % 2 == 0:
+def add_bias(nc, on_vector, dest, acc, bias_col, relu):
+    if not on_vector:
         nc.scalar.activation(dest, acc, RELU if relu else IDENTITY, bias=bias_col)
     elif relu:
         nc.vector.tensor_scalar(dest, acc, bias_col, 0.0, ADD, MAX)
@@ -97,6 +98,7 @@ def tile_efficientrelationshipmodel_b_kernel(
             col = first_col[name] + block
             return bias_cols[:, col : col + 1]
 
+
         a = []
         for half, (w1_sb, b1) in enumerate(((ws1_sb, "bs1"), (we1_sb, "be1"))):
             picked = table_sb[:].indirect(offsets[:, half * (E // 16) : (half + 1) * (E // 16)])
@@ -105,7 +107,7 @@ def tile_efficientrelationshipmodel_b_kernel(
                 acc = psum.tile([P, E], F32, name="acc")
                 nc.tensor.matmul(acc[:], w1_sb[:, 0, m * P : (m + 1) * P], picked, start=True, stop=True)
                 a_block = held.tile([P, E], BF16, name=f"a{half}_{m}")
-                add_bias(nc, m, a_block[:], acc[:], bias(b1, m), relu=True)
+                add_bias(nc, m % 2 == 1, a_block[:], acc[:], bias(b1, m), relu=True)
                 a[half].append(a_block)
 
         cat = []
@@ -113,14 +115,14 @@ def tile_efficientrelationshipmodel_b_kernel(
             for m in range(H // P):
                 acc = project(nc, psum, w2_sb, 0, a[half], m)
                 cat_block = held.tile([P, E], BF16, name=f"cat{half}_{m}")
-                add_bias(nc, m, cat_block[:], acc[:], bias(b2, m), relu=True)
+                add_bias(nc, m % 2 == 1, cat_block[:], acc[:], bias(b2, m), relu=True)
                 cat.append(cat_block)
 
         ent = []
         for m in range(EO // P):
             acc = project(nc, psum, wo_sb, 0, cat, m)
             ent_block = held.tile([P, E], BF16, name=f"ent{m}")
-            add_bias(nc, m, ent_block[:], acc[:], bias("bo", m), relu=False)
+            add_bias(nc, m % 2 == 1, ent_block[:], acc[:], bias("bo", m), relu=False)
             ent.append(ent_block)
 
         hp = []
@@ -153,7 +155,9 @@ def tile_efficientrelationshipmodel_b_kernel(
                 at = column % STORE
                 for d in range(DO // P):
                     acc = project(nc, psum, wr2_sb, 0, hid, d)
-                    nc.scalar.activation(staged[d][:, at : at + E], acc[:], IDENTITY, bias=bias("br2", d))
+                    bank = (column // E) * (DO // P) + d
+                    on_vector = bank % VECTOR_DRAINS == VECTOR_DRAINS - 1
+                    add_bias(nc, on_vector, staged[d][:, at : at + E], acc[:], bias("br2", d), relu=False)
                 width = E if column >= B * NE * NE - STORE else STORE
                 if (column + E) % width == 0:
                     for d in range(DO // P):

@@ -18,9 +18,9 @@ R = 256
 DO = 256
 B = 8
 NE = 64
-FIRSTS = E // NE
 STORE = 2048
-VECTOR_DRAINS = 8
+BANKS = 8
+AHEAD = 2
 
 FLOPS = 2 * (P * H * 2 * E + 2 * H * H * E + EO * EO * E + 2 * EO * R * E + R * DO * B * NE * NE)
 
@@ -34,12 +34,16 @@ def add_bias(nc, on_vector, dest, acc, bias_col, relu):
         nc.vector.tensor_scalar_add(dest, acc, bias_col)
 
 
-def project(nc, psum, weights, first_k, moving, m):
-    acc = psum.tile([P, E], F32, name="acc")
+def project(nc, bank, weights, first_k, moving, m, at, width):
+    acc = bank[:, 0:width]
     last = len(moving) - 1
     for k, block in enumerate(moving):
         nc.tensor.matmul(
-            acc[:], weights[:, first_k + k, m * P : (m + 1) * P], block[:], start=(k == 0), stop=(k == last)
+            acc,
+            weights[:, first_k + k, m * P : (m + 1) * P],
+            block[:, at : at + width],
+            start=(k == 0),
+            stop=(k == last),
         )
     return acc
 
@@ -50,10 +54,12 @@ def tile_efficientrelationshipmodel_b_kernel(
     nc = tc.nc
     with (
         tc.tile_pool(name="held", bufs=1) as held,
-        tc.tile_pool(name="pairs", bufs=4) as pairs,
-        tc.tile_pool(name="staging", bufs=3) as staging,
-        tc.psum_pool(name="psum", bufs=8) as psum,
+        tc.tile_pool(name="pairs", bufs=(AHEAD + 1) * (STORE // E)) as pairs,
+        tc.tile_pool(name="staging", bufs=6) as staging,
+        tc.psum_pool(name="psum", bufs=1) as psum,
     ):
+        banks = [psum.tile([P, E], F32, name=f"bank{b}") for b in range(BANKS)]
+
         offsets = held.tile([P, 2 * E // 16], U16, name="offsets")
         nc.sync.dma_start(offsets[:], offs)
 
@@ -89,10 +95,10 @@ def tile_efficientrelationshipmodel_b_kernel(
 
         identity = held.tile([P, P], F32, name="identity")
         make_identity(nc, identity[:])
-        flipped = psum.tile([P, E], F32, name="acc")
-        nc.tensor.transpose(flipped[:, 0:P], bias_rows[:], identity[:])
+        flipped = banks[BANKS - 1][:, 0:P]
+        nc.tensor.transpose(flipped, bias_rows[:], identity[:])
         bias_cols = held.tile([P, P], F32, name="bias_cols")
-        nc.vector.tensor_copy(bias_cols[:], flipped[:, 0:P])
+        nc.vector.tensor_copy(bias_cols[:], flipped)
 
         def bias(name, block):
             col = first_col[name] + block
@@ -104,64 +110,66 @@ def tile_efficientrelationshipmodel_b_kernel(
             picked = table_sb[:].indirect(offsets[:, half * (E // 16) : (half + 1) * (E // 16)])
             a.append([])
             for m in range(H // P):
-                acc = psum.tile([P, E], F32, name="acc")
-                nc.tensor.matmul(acc[:], w1_sb[:, 0, m * P : (m + 1) * P], picked, start=True, stop=True)
+                bank = banks[half * (H // P) + m]
+                nc.tensor.matmul(bank[:], w1_sb[:, 0, m * P : (m + 1) * P], picked, start=True, stop=True)
                 a_block = held.tile([P, E], BF16, name=f"a{half}_{m}")
-                add_bias(nc, m % 2 == 1, a_block[:], acc[:], bias(b1, m), relu=True)
+                add_bias(nc, m % 2 == 1, a_block[:], bank[:], bias(b1, m), relu=True)
                 a[half].append(a_block)
 
         cat = []
         for half, (w2_sb, b2) in enumerate(((ws2_sb, "bs2"), (we2_sb, "be2"))):
             for m in range(H // P):
-                acc = project(nc, psum, w2_sb, 0, a[half], m)
+                acc = project(nc, banks[half * (H // P) + m], w2_sb, 0, a[half], m, 0, E)
                 cat_block = held.tile([P, E], BF16, name=f"cat{half}_{m}")
-                add_bias(nc, m % 2 == 1, cat_block[:], acc[:], bias(b2, m), relu=True)
+                add_bias(nc, m % 2 == 1, cat_block[:], acc, bias(b2, m), relu=True)
                 cat.append(cat_block)
 
         ent = []
         for m in range(EO // P):
-            acc = project(nc, psum, wo_sb, 0, cat, m)
+            acc = project(nc, banks[m], wo_sb, 0, cat, m, 0, E)
             ent_block = held.tile([P, E], BF16, name=f"ent{m}")
-            add_bias(nc, m % 2 == 1, ent_block[:], acc[:], bias("bo", m), relu=False)
+            add_bias(nc, m % 2 == 1, ent_block[:], acc, bias("bo", m), relu=False)
             ent.append(ent_block)
 
         hp = []
         hq = []
-        for m in range(R // P):
-            acc = project(nc, psum, wr1_sb, 0, ent, m)
-            hp_block = held.tile([P, E], F32, name=f"hp{m}")
-            nc.scalar.activation(hp_block[:], acc[:], IDENTITY, bias=bias("br1", m))
-            hp.append(hp_block)
-            acc = project(nc, psum, wr1_sb, EO // P, ent, m)
-            hq_block = held.tile([P, E], F32, name=f"hq{m}")
-            nc.vector.tensor_copy(hq_block[:], acc[:])
-            hq.append(hq_block)
+        for half in range(2):
+            hp.append([held.tile([P, E // 2], F32, name=f"hp{half}_{m}") for m in range(R // P)])
+            hq.append([held.tile([P, E // 2], F32, name=f"hq{half}_{m}") for m in range(R // P)])
+            for m in range(R // P):
+                bank = 4 * half + 2 * m
+                acc = project(nc, banks[bank], wr1_sb, 0, ent, m, half * (E // 2), E // 2)
+                nc.scalar.activation(hp[half][m][:], acc, IDENTITY, bias=bias("br1", m))
+                acc = project(nc, banks[bank + 1], wr1_sb, EO // P, ent, m, half * (E // 2), E // 2)
+                nc.scalar.copy(hq[half][m][:], acc)
 
-        for u in range(B):
-            seconds = slice(u * NE, (u + 1) * NE)
-            for group in range(NE // FIRSTS):
-                column = (u * NE + group * FIRSTS) * NE
-                hid = []
-                for m in range(R // P):
-                    hid_block = pairs.tile([P, E], BF16, name=f"hid{m}")
-                    for i in range(FIRSTS):
-                        p = u * NE + group * FIRSTS + i
+        def make_hid(window):
+            banks = []
+            for c in range(STORE // E):
+                hid = [pairs.tile([P, E], BF16, name=f"hid{m}") for m in range(R // P)]
+                for i in range(E // NE):
+                    half, p = divmod(window * (STORE // NE) + c * (E // NE) + i, E // 2)
+                    batch = p // NE
+                    for m in range(R // P):
                         nc.vector.tensor_scalar(
-                            hid_block[:, i * NE : (i + 1) * NE], hq[m][:, seconds], hp[m][:, p : p + 1], 0.0, ADD, MAX
+                            hid[m][:, i * NE : (i + 1) * NE],
+                            hq[half][m][:, batch * NE : (batch + 1) * NE],
+                            hp[half][m][:, p : p + 1],
+                            0.0,
+                            ADD,
+                            MAX,
                         )
-                    hid.append(hid_block)
-                if column % STORE == 0:
-                    staged = [staging.tile([P, STORE], F32, name=f"staged{d}") for d in range(DO // P)]
-                at = column % STORE
-                for d in range(DO // P):
-                    acc = project(nc, psum, wr2_sb, 0, hid, d)
-                    bank = (column // E) * (DO // P) + d
-                    on_vector = bank % VECTOR_DRAINS == VECTOR_DRAINS - 1
-                    add_bias(nc, on_vector, staged[d][:, at : at + E], acc[:], bias("br2", d), relu=False)
-                width = E if column >= B * NE * NE - STORE else STORE
-                if (column + E) % width == 0:
-                    for d in range(DO // P):
-                        nc.sync.dma_start(
-                            out[d * P : (d + 1) * P, column + E - width : column + E],
-                            staged[d][:, at + E - width : at + E],
-                        )
+                banks.append(hid)
+            return banks
+
+        windows = B * NE * NE // STORE
+        hid_of = [make_hid(window) for window in range(AHEAD)]
+        for window in range(windows):
+            for d in range(DO // P):
+                staged = staging.tile([P, STORE], F32, name="staged")
+                for c in range(STORE // E):
+                    acc = project(nc, banks[d * (STORE // E) + c], wr2_sb, 0, hid_of[window][c], d, 0, E)
+                    add_bias(nc, False, staged[:, c * E : (c + 1) * E], acc, bias("br2", d), relu=False)
+                nc.sync.dma_start(out[d * P : (d + 1) * P, window * STORE : (window + 1) * STORE], staged[:])
+            if window + AHEAD < windows:
+                hid_of.append(make_hid(window + AHEAD))

@@ -20,6 +20,7 @@ B = 8
 NE = 64
 STORE = 2048
 BANKS = 8
+WARM_UP = 12
 AHEAD = 2
 
 FLOPS = 2 * (P * H * 2 * E + 2 * H * H * E + EO * EO * E + 2 * EO * R * E + R * DO * B * NE * NE)
@@ -59,6 +60,11 @@ def tile_efficientrelationshipmodel_b_kernel(
         tc.psum_pool(name="psum", bufs=1) as psum,
     ):
         banks = [psum.tile([P, E], F32, name=f"bank{b}") for b in range(BANKS)]
+
+        zeros = held.tile([P, E], BF16, name="zeros")
+        nc.vector.memset(zeros[:], 0.0)
+        for i in range(WARM_UP):
+            nc.tensor.matmul(banks[0][:], zeros[:, 0:P], zeros[:], start=True, stop=True)
 
         offsets = held.tile([P, 2 * E // 16], U16, name="offsets")
         nc.sync.dma_start(offsets[:], offs)
@@ -167,9 +173,15 @@ def tile_efficientrelationshipmodel_b_kernel(
         for window in range(windows):
             for d in range(DO // P):
                 staged = staging.tile([P, STORE], F32, name="staged")
+                piece = E if (window == windows - 1 and d == DO // P - 1) else STORE
                 for c in range(STORE // E):
                     acc = project(nc, banks[d * (STORE // E) + c], wr2_sb, 0, hid_of[window][c], d, 0, E)
                     add_bias(nc, False, staged[:, c * E : (c + 1) * E], acc, bias("br2", d), relu=False)
-                nc.sync.dma_start(out[d * P : (d + 1) * P, window * STORE : (window + 1) * STORE], staged[:])
+                    drained = (c + 1) * E
+                    if drained % piece == 0:
+                        nc.sync.dma_start(
+                            out[d * P : (d + 1) * P, window * STORE + drained - piece : window * STORE + drained],
+                            staged[:, drained - piece : drained],
+                        )
             if window + AHEAD < windows:
                 hid_of.append(make_hid(window + AHEAD))

@@ -173,15 +173,9 @@ def tile_efficientrelationshipmodel_b_kernel(
         for window in range(windows):
             for d in range(DO // P):
                 staged = staging.tile([P, STORE], F32, name="staged")
-                piece = E if (window == windows - 1 and d == DO // P - 1) else STORE
                 for c in range(STORE // E):
                     acc = project(nc, banks[d * (STORE // E) + c], wr2_sb, 0, hid_of[window][c], d, 0, E)
                     add_bias(nc, False, staged[:, c * E : (c + 1) * E], acc, bias("br2", d), relu=False)
-                    drained = (c + 1) * E
-                    if drained % piece == 0:
-                        nc.sync.dma_start(
-                            out[d * P : (d + 1) * P, window * STORE + drained - piece : window * STORE + drained],
-                            staged[:, drained - piece : drained],
-                        )
+                nc.sync.dma_start(out[d * P : (d + 1) * P, window * STORE : (window + 1) * STORE], staged[:])
             if window + AHEAD < windows:
                 hid_of.append(make_hid(window + AHEAD))

@@ -175,7 +175,8 @@ def tile_efficientrelationshipmodel_b_kernel(
                 staged = staging.tile([P, STORE], F32, name="staged")
                 for c in range(STORE // E):
                     acc = project(nc, banks[d * (STORE // E) + c], wr2_sb, 0, hid_of[window][c], d, 0, E)
-                    add_bias(nc, False, staged[:, c * E : (c + 1) * E], acc, bias("br2", d), relu=False)
+                    last_of_window = d == DO // P - 1 and c == STORE // E - 1
+                    add_bias(nc, last_of_window, staged[:, c * E : (c + 1) * E], acc, bias("br2", d), relu=False)
                 nc.sync.dma_start(out[d * P : (d + 1) * P, window * STORE : (window + 1) * STORE], staged[:])
             if window + AHEAD < windows:
                 hid_of.append(make_hid(window + AHEAD))

@@ -12,6 +12,7 @@ IDENTITY = mybir.ActivationFunctionType.Identity
 P = 128
 S = 4096
 E = 512
+HALF = E // 2
 H = 512
 EO = 1024
 R = 256
@@ -21,7 +22,7 @@ NE = 64
 STORE = 2048
 BANKS = 8
 WARM_UP = 12
-AHEAD = 2
+AHEAD = 5
 
 FLOPS = 2 * (P * H * 2 * E + 2 * H * H * E + EO * EO * E + 2 * EO * R * E + R * DO * B * NE * NE)
 
@@ -60,6 +61,11 @@ def tile_efficientrelationshipmodel_b_kernel(
         tc.psum_pool(name="psum", bufs=1) as psum,
     ):
         banks = [psum.tile([P, E], F32, name=f"bank{b}") for b in range(BANKS)]
+        taken = []
+
+        def next_bank():
+            taken.append(len(taken))
+            return banks[taken[-1] % BANKS]
 
         zeros = held.tile([P, E], BF16, name="zeros")
         nc.vector.memset(zeros[:], 0.0)
@@ -110,51 +116,57 @@ def tile_efficientrelationshipmodel_b_kernel(
             col = first_col[name] + block
             return bias_cols[:, col : col + 1]
 
-
         a = []
-        for half, (w1_sb, b1) in enumerate(((ws1_sb, "bs1"), (we1_sb, "be1"))):
-            picked = table_sb[:].indirect(offsets[:, half * (E // 16) : (half + 1) * (E // 16)])
+        for side, (w1_sb, b1) in enumerate(((ws1_sb, "bs1"), (we1_sb, "be1"))):
+            picked = table_sb[:].indirect(offsets[:, side * (E // 16) : (side + 1) * (E // 16)])
             a.append([])
             for m in range(H // P):
-                bank = banks[half * (H // P) + m]
+                bank = next_bank()
                 nc.tensor.matmul(bank[:], w1_sb[:, 0, m * P : (m + 1) * P], picked, start=True, stop=True)
-                a_block = held.tile([P, E], BF16, name=f"a{half}_{m}")
+                a_block = held.tile([P, E], BF16, name=f"a{side}_{m}")
                 add_bias(nc, m % 2 == 1, a_block[:], bank[:], bias(b1, m), relu=True)
-                a[half].append(a_block)
+                a[side].append(a_block)
 
-        cat = []
-        for half, (w2_sb, b2) in enumerate(((ws2_sb, "bs2"), (we2_sb, "be2"))):
-            for m in range(H // P):
-                acc = project(nc, banks[half * (H // P) + m], w2_sb, 0, a[half], m, 0, E)
-                cat_block = held.tile([P, E], BF16, name=f"cat{half}_{m}")
-                add_bias(nc, m % 2 == 1, cat_block[:], acc, bias(b2, m), relu=True)
-                cat.append(cat_block)
+        cat = [[], []]
+        ent = [[], []]
+        hp = [[], []]
+        hq = [[], []]
 
-        ent = []
-        for m in range(EO // P):
-            acc = project(nc, banks[m], wo_sb, 0, cat, m, 0, E)
-            ent_block = held.tile([P, E], BF16, name=f"ent{m}")
-            add_bias(nc, m % 2 == 1, ent_block[:], acc, bias("bo", m), relu=False)
-            ent.append(ent_block)
+        def odd_on_vector(half, m):
+            return half == 0 and m % 2 == 1
 
-        hp = []
-        hq = []
-        for half in range(2):
-            hp.append([held.tile([P, E // 2], F32, name=f"hp{half}_{m}") for m in range(R // P)])
-            hq.append([held.tile([P, E // 2], F32, name=f"hq{half}_{m}") for m in range(R // P)])
+        def stage2(half):
+            for side, (w2_sb, b2) in enumerate(((ws2_sb, "bs2"), (we2_sb, "be2"))):
+                for m in range(H // P):
+                    acc = project(nc, next_bank(), w2_sb, 0, a[side], m, half * HALF, HALF)
+                    cat_block = held.tile([P, HALF], BF16, name=f"cat{half}_{side}_{m}")
+                    add_bias(nc, odd_on_vector(half, m), cat_block[:], acc, bias(b2, m), relu=True)
+                    cat[half].append(cat_block)
+
+        def stage3(half, blocks):
+            for m in blocks:
+                acc = project(nc, next_bank(), wo_sb, 0, cat[half], m, 0, HALF)
+                ent_block = held.tile([P, HALF], BF16, name=f"ent{half}_{m}")
+                add_bias(nc, odd_on_vector(half, m), ent_block[:], acc, bias("bo", m), relu=False)
+                ent[half].append(ent_block)
+
+        def stage4(half):
             for m in range(R // P):
-                bank = 4 * half + 2 * m
-                acc = project(nc, banks[bank], wr1_sb, 0, ent, m, half * (E // 2), E // 2)
-                nc.scalar.activation(hp[half][m][:], acc, IDENTITY, bias=bias("br1", m))
-                acc = project(nc, banks[bank + 1], wr1_sb, EO // P, ent, m, half * (E // 2), E // 2)
-                nc.scalar.copy(hq[half][m][:], acc)
+                hp_block = held.tile([P, HALF], F32, name=f"hp{half}_{m}")
+                acc = project(nc, next_bank(), wr1_sb, 0, ent[half], m, 0, HALF)
+                nc.scalar.activation(hp_block[:], acc, IDENTITY, bias=bias("br1", m))
+                hp[half].append(hp_block)
+                hq_block = held.tile([P, HALF], F32, name=f"hq{half}_{m}")
+                acc = project(nc, next_bank(), wr1_sb, EO // P, ent[half], m, 0, HALF)
+                nc.scalar.copy(hq_block[:], acc)
+                hq[half].append(hq_block)
 
         def make_hid(window):
-            banks = []
+            hid_banks = []
             for c in range(STORE // E):
                 hid = [pairs.tile([P, E], BF16, name=f"hid{m}") for m in range(R // P)]
                 for i in range(E // NE):
-                    half, p = divmod(window * (STORE // NE) + c * (E // NE) + i, E // 2)
+                    half, p = divmod(window * (STORE // NE) + c * (E // NE) + i, HALF)
                     batch = p // NE
                     for m in range(R // P):
                         nc.vector.tensor_scalar(
@@ -165,18 +177,35 @@ def tile_efficientrelationshipmodel_b_kernel(
                             ADD,
                             MAX,
                         )
-                banks.append(hid)
-            return banks
+                hid_banks.append(hid)
+            return hid_banks
+
+        def make_out(window, hid_banks, vector_helps):
+            for d in range(DO // P):
+                staged = staging.tile([P, STORE], F32, name="staged")
+                for c in range(STORE // E):
+                    acc = project(nc, next_bank(), wr2_sb, 0, hid_banks[c], d, 0, E)
+                    add_bias(
+                        nc, vector_helps and d == 0, staged[:, c * E : (c + 1) * E], acc, bias("br2", d), relu=False
+                    )
+                nc.sync.dma_start(out[d * P : (d + 1) * P, window * STORE : (window + 1) * STORE], staged[:])
+
+        stage2(0)
+        stage3(0, range(EO // P))
+        stage4(0)
+
+        pieces = (
+            lambda: stage2(1),
+            lambda: stage3(1, range(0, EO // P // 2)),
+            lambda: stage3(1, range(EO // P // 2, EO // P)),
+            lambda: stage4(1),
+        )
 
         windows = B * NE * NE // STORE
         hid_of = [make_hid(window) for window in range(AHEAD)]
         for window in range(windows):
-            for d in range(DO // P):
-                staged = staging.tile([P, STORE], F32, name="staged")
-                for c in range(STORE // E):
-                    acc = project(nc, banks[d * (STORE // E) + c], wr2_sb, 0, hid_of[window][c], d, 0, E)
-                    last_of_window = d == DO // P - 1 and c == STORE // E - 1
-                    add_bias(nc, last_of_window, staged[:, c * E : (c + 1) * E], acc, bias("br2", d), relu=False)
-                nc.sync.dma_start(out[d * P : (d + 1) * P, window * STORE : (window + 1) * STORE], staged[:])
+            if window < len(pieces):
+                pieces[window]()
+            make_out(window, hid_of[window], vector_helps=(window + AHEAD >= windows))
             if window + AHEAD < windows:
                 hid_of.append(make_hid(window + AHEAD))

@@ -72,8 +72,17 @@ def tile_efficientrelationshipmodel_b_kernel(
         for i in range(WARM_UP):
             nc.tensor.matmul(banks[0][:], zeros[:, 0:P], zeros[:], start=True, stop=True)
 
+        def load_blocks(name, weights):
+            rows, columns = weights.shape
+            tile = held.tile([P, rows // P, columns], BF16, name=name)
+            nc.sync.dma_start(tile[:], weights.rearrange("(k p) c -> p k c", p=P))
+            return tile
+
         offsets = held.tile([P, 2 * E // 16], U16, name="offsets")
         nc.sync.dma_start(offsets[:], offs)
+        ws1_sb = load_blocks("ws1_sb", ws1)
+        table_sb = held.tile([P, S], BF16, name="table_sb")
+        nc.sync.dma_start(table_sb[:], table)
 
         bias_rows = held.tile([P, P], F32, name="bias_rows")
         nc.gpsimd.memset(bias_rows[:], 0.0)
@@ -89,15 +98,6 @@ def tile_efficientrelationshipmodel_b_kernel(
             first_col[name] = rows_used
             rows_used += blocks
 
-        def load_blocks(name, weights):
-            rows, columns = weights.shape
-            tile = held.tile([P, rows // P, columns], BF16, name=name)
-            nc.sync.dma_start(tile[:], weights.rearrange("(k p) c -> p k c", p=P))
-            return tile
-
-        ws1_sb = load_blocks("ws1_sb", ws1)
-        table_sb = held.tile([P, S], BF16, name="table_sb")
-        nc.sync.dma_start(table_sb[:], table)
         we1_sb = load_blocks("we1_sb", we1)
         ws2_sb = load_blocks("ws2_sb", ws2)
         we2_sb = load_blocks("we2_sb", we2)

@@ -21,7 +21,6 @@ B = 8
 NE = 64
 STORE = 2048
 BANKS = 8
-WARM_UP = 12
 AHEAD = 5
 
 FLOPS = 2 * (P * H * 2 * E + 2 * H * H * E + EO * EO * E + 2 * EO * R * E + R * DO * B * NE * NE)
@@ -66,11 +65,6 @@ def tile_efficientrelationshipmodel_b_kernel(
         def next_bank():
             taken.append(len(taken))
             return banks[taken[-1] % BANKS]
-
-        zeros = held.tile([P, E], BF16, name="zeros")
-        nc.vector.memset(zeros[:], 0.0)
-        for i in range(WARM_UP):
-            nc.tensor.matmul(banks[0][:], zeros[:, 0:P], zeros[:], start=True, stop=True)
 
         def load_blocks(name, weights):
             rows, columns = weights.shape

@@ -180,7 +180,7 @@ def tile_efficientrelationshipmodel_b_kernel(
                 for c in range(STORE // E):
                     acc = project(nc, next_bank(), wr2_sb, 0, hid_banks[c], d, 0, E)
                     add_bias(
-                        nc, vector_helps and d == 0, staged[:, c * E : (c + 1) * E], acc, bias("br2", d), relu=False
+                        nc, vector_helps and c < 2, staged[:, c * E : (c + 1) * E], acc, bias("br2", d), relu=False
                     )
                 nc.sync.dma_start(out[d * P : (d + 1) * P, window * STORE : (window + 1) * STORE], staged[:])
 

@@ -12,16 +12,17 @@ IDENTITY = mybir.ActivationFunctionType.Identity
 P = 128
 S = 4096
 E = 512
-HALF = E // 2
 H = 512
 EO = 1024
 R = 256
 DO = 256
 B = 8
 NE = 64
+GROUPS = (3, 3, 2)
 STORE = 2048
 BANKS = 8
-AHEAD = 5
+AHEAD = 3
+HELPED = 2
 
 FLOPS = 2 * (P * H * 2 * E + 2 * H * H * E + EO * EO * E + 2 * EO * R * E + R * DO * B * NE * NE)
 
@@ -121,52 +122,62 @@ def tile_efficientrelationshipmodel_b_kernel(
                 add_bias(nc, m % 2 == 1, a_block[:], bank[:], bias(b1, m), relu=True)
                 a[side].append(a_block)
 
-        cat = [[], []]
-        ent = [[], []]
-        hp = [[], []]
-        hq = [[], []]
+        widths = [batches * NE for batches in GROUPS]
+        starts = [sum(widths[:g]) for g in range(len(GROUPS))]
+        cat = [[] for g in GROUPS]
+        ent = [[] for g in GROUPS]
+        hp = [[] for g in GROUPS]
+        hq = [[] for g in GROUPS]
 
-        def odd_on_vector(half, m):
-            return half == 0 and m % 2 == 1
+        def odd_on_vector(g, m):
+            return g == 0 and m % 2 == 1
 
-        def stage2(half):
-            for side, (w2_sb, b2) in enumerate(((ws2_sb, "bs2"), (we2_sb, "be2"))):
-                for m in range(H // P):
-                    acc = project(nc, next_bank(), w2_sb, 0, a[side], m, half * HALF, HALF)
-                    cat_block = held.tile([P, HALF], BF16, name=f"cat{half}_{side}_{m}")
-                    add_bias(nc, odd_on_vector(half, m), cat_block[:], acc, bias(b2, m), relu=True)
-                    cat[half].append(cat_block)
+        def stage2(g, side):
+            w2_sb, b2 = ((ws2_sb, "bs2"), (we2_sb, "be2"))[side]
+            for m in range(H // P):
+                acc = project(nc, next_bank(), w2_sb, 0, a[side], m, starts[g], widths[g])
+                cat_block = held.tile([P, widths[g]], BF16, name=f"cat{g}_{side}_{m}")
+                add_bias(nc, odd_on_vector(g, m), cat_block[:], acc, bias(b2, m), relu=True)
+                cat[g].append(cat_block)
 
-        def stage3(half, blocks):
+        def stage3(g, blocks):
             for m in blocks:
-                acc = project(nc, next_bank(), wo_sb, 0, cat[half], m, 0, HALF)
-                ent_block = held.tile([P, HALF], BF16, name=f"ent{half}_{m}")
-                add_bias(nc, odd_on_vector(half, m), ent_block[:], acc, bias("bo", m), relu=False)
-                ent[half].append(ent_block)
+                acc = project(nc, next_bank(), wo_sb, 0, cat[g], m, 0, widths[g])
+                ent_block = held.tile([P, widths[g]], BF16, name=f"ent{g}_{m}")
+                add_bias(nc, odd_on_vector(g, m), ent_block[:], acc, bias("bo", m), relu=False)
+                ent[g].append(ent_block)
 
-        def stage4(half):
-            for m in range(R // P):
-                hp_block = held.tile([P, HALF], F32, name=f"hp{half}_{m}")
-                acc = project(nc, next_bank(), wr1_sb, 0, ent[half], m, 0, HALF)
-                nc.scalar.activation(hp_block[:], acc, IDENTITY, bias=bias("br1", m))
-                hp[half].append(hp_block)
-                hq_block = held.tile([P, HALF], F32, name=f"hq{half}_{m}")
-                acc = project(nc, next_bank(), wr1_sb, EO // P, ent[half], m, 0, HALF)
-                nc.scalar.copy(hq_block[:], acc)
-                hq[half].append(hq_block)
+        def stage4(g, m):
+            hp_block = held.tile([P, widths[g]], F32, name=f"hp{g}_{m}")
+            acc = project(nc, next_bank(), wr1_sb, 0, ent[g], m, 0, widths[g])
+            nc.scalar.activation(hp_block[:], acc, IDENTITY, bias=bias("br1", m))
+            hp[g].append(hp_block)
+            hq_block = held.tile([P, widths[g]], F32, name=f"hq{g}_{m}")
+            acc = project(nc, next_bank(), wr1_sb, EO // P, ent[g], m, 0, widths[g])
+            nc.scalar.copy(hq_block[:], acc)
+            hq[g].append(hq_block)
+
+        def pieces_of(g):
+            calls = [lambda side=side: stage2(g, side) for side in range(2)]
+            calls += [lambda m=m: stage3(g, (m, m + 1)) for m in range(0, EO // P, 2)]
+            calls += [lambda m=m: stage4(g, m) for m in range(R // P)]
+            return calls
+
+        group_of = [g for g, batches in enumerate(GROUPS) for w in range(batches * NE * NE // STORE)]
 
         def make_hid(window):
+            g = group_of[window]
             hid_banks = []
             for c in range(STORE // E):
                 hid = [pairs.tile([P, E], BF16, name=f"hid{m}") for m in range(R // P)]
                 for i in range(E // NE):
-                    half, p = divmod(window * (STORE // NE) + c * (E // NE) + i, HALF)
+                    p = window * (STORE // NE) + c * (E // NE) + i - starts[g]
                     batch = p // NE
                     for m in range(R // P):
                         nc.vector.tensor_scalar(
                             hid[m][:, i * NE : (i + 1) * NE],
-                            hq[half][m][:, batch * NE : (batch + 1) * NE],
-                            hp[half][m][:, p : p + 1],
+                            hq[g][m][:, batch * NE : (batch + 1) * NE],
+                            hp[g][m][:, p : p + 1],
                             0.0,
                             ADD,
                             MAX,
@@ -184,22 +195,21 @@ def tile_efficientrelationshipmodel_b_kernel(
                     )
                 nc.sync.dma_start(out[d * P : (d + 1) * P, window * STORE : (window + 1) * STORE], staged[:])
 
-        stage2(0)
-        stage3(0, range(EO // P))
-        stage4(0)
+        for piece in pieces_of(0):
+            piece()
 
-        pieces = (
-            lambda: stage2(1),
-            lambda: stage3(1, range(0, EO // P // 2)),
-            lambda: stage3(1, range(EO // P // 2, EO // P)),
-            lambda: stage4(1),
-        )
+        before = {}
+        for g in range(1, len(GROUPS)):
+            pieces = pieces_of(g)
+            own = [window for window, owner in enumerate(group_of) if owner == g - 1]
+            for i, piece in enumerate(pieces):
+                before.setdefault(own[i * (len(own) - 1) // len(pieces)], []).append(piece)
 
-        windows = B * NE * NE // STORE
-        hid_of = [make_hid(window) for window in range(AHEAD)]
+        windows = len(group_of)
+        hid_of = []
         for window in range(windows):
-            if window < len(pieces):
-                pieces[window]()
-            make_out(window, hid_of[window], vector_helps=(window + AHEAD >= windows))
-            if window + AHEAD < windows:
-                hid_of.append(make_hid(window + AHEAD))
+            for piece in before.get(window, []):
+                piece()
+            while len(hid_of) < min(window + 1 + AHEAD, windows) and len(hq[group_of[len(hid_of)]]) == R // P:
+                hid_of.append(make_hid(len(hid_of)))
+            make_out(window, hid_of[window], vector_helps=(window + HELPED >= windows))

@@ -18,7 +18,7 @@ R = 256
 DO = 256
 B = 8
 NE = 64
-GROUPS = (3, 3, 2)
+GROUPS = (5, 3)
 STORE = 2048
 BANKS = 8
 AHEAD = 3
@@ -188,12 +188,16 @@ def tile_efficientrelationshipmodel_b_kernel(
         def make_out(window, hid_banks, vector_helps):
             for d in range(DO // P):
                 staged = staging.tile([P, STORE], F32, name="staged")
+                rows = out[d * P : (d + 1) * P, window * STORE : (window + 1) * STORE]
                 for c in range(STORE // E):
                     acc = project(nc, next_bank(), wr2_sb, 0, hid_banks[c], d, 0, E)
                     add_bias(
                         nc, vector_helps and c < 2, staged[:, c * E : (c + 1) * E], acc, bias("br2", d), relu=False
                     )
-                nc.sync.dma_start(out[d * P : (d + 1) * P, window * STORE : (window + 1) * STORE], staged[:])
+                parts = 2 if window == len(group_of) - 1 and d == DO // P - 1 else 1
+                for part in range(parts):
+                    columns = slice(part * STORE // parts, (part + 1) * STORE // parts)
+                    nc.sync.dma_start(rows[:, columns], staged[:, columns])
 
         for piece in pieces_of(0):
             piece()

@@ -18,7 +18,7 @@ R = 256
 DO = 256
 B = 8
 NE = 64
-GROUPS = (5, 3)
+GROUPS = (4, 4)
 STORE = 2048
 BANKS = 8
 AHEAD = 3
@@ -154,7 +154,10 @@ def tile_efficientrelationshipmodel_b_kernel(
             hp[g].append(hp_block)
             hq_block = held.tile([P, widths[g]], F32, name=f"hq{g}_{m}")
             acc = project(nc, next_bank(), wr1_sb, EO // P, ent[g], m, 0, widths[g])
-            nc.scalar.copy(hq_block[:], acc)
+            if g == 0:
+                nc.vector.tensor_copy(hq_block[:], acc)
+            else:
+                nc.scalar.copy(hq_block[:], acc)
             hq[g].append(hq_block)
 
         def pieces_of(g):
@@ -188,16 +191,12 @@ def tile_efficientrelationshipmodel_b_kernel(
         def make_out(window, hid_banks, vector_helps):
             for d in range(DO // P):
                 staged = staging.tile([P, STORE], F32, name="staged")
-                rows = out[d * P : (d + 1) * P, window * STORE : (window + 1) * STORE]
                 for c in range(STORE // E):
                     acc = project(nc, next_bank(), wr2_sb, 0, hid_banks[c], d, 0, E)
                     add_bias(
                         nc, vector_helps and c < 2, staged[:, c * E : (c + 1) * E], acc, bias("br2", d), relu=False
                     )
-                parts = 2 if window == len(group_of) - 1 and d == DO // P - 1 else 1
-                for part in range(parts):
-                    columns = slice(part * STORE // parts, (part + 1) * STORE // parts)
-                    nc.sync.dma_start(rows[:, columns], staged[:, columns])
+                nc.sync.dma_start(out[d * P : (d + 1) * P, window * STORE : (window + 1) * STORE], staged[:])
 
         for piece in pieces_of(0):
             piece()
@@ -206,8 +205,9 @@ def tile_efficientrelationshipmodel_b_kernel(
         for g in range(1, len(GROUPS)):
             pieces = pieces_of(g)
             own = [window for window, owner in enumerate(group_of) if owner == g - 1]
-            for i, piece in enumerate(pieces):
-                before.setdefault(own[i * (len(own) - 1) // len(pieces)], []).append(piece)
+            before[own[0]] = pieces[:2]
+            for i, piece in enumerate(pieces[2:]):
+                before.setdefault(own[1 + i * (len(own) - 2) // len(pieces[2:])], []).append(piece)
 
         windows = len(group_of)
         hid_of = []

@@ -19,6 +19,7 @@ DO = 256
 B = 8
 NE = 64
 GROUPS = (4, 4)
+BIAS_ROWS = 64
 STORE = 2048
 BANKS = 8
 AHEAD = 3
@@ -79,7 +80,7 @@ def tile_efficientrelationshipmodel_b_kernel(
         table_sb = held.tile([P, S], BF16, name="table_sb")
         nc.sync.dma_start(table_sb[:], table)
 
-        bias_rows = held.tile([P, P], F32, name="bias_rows")
+        bias_rows = held.tile([BIAS_ROWS, P], F32, name="bias_rows")
         nc.gpsimd.memset(bias_rows[:], 0.0)
         first_col = {}
         rows_used = 0
@@ -100,11 +101,11 @@ def tile_efficientrelationshipmodel_b_kernel(
         wr1_sb = load_blocks("wr1_sb", wr1)
         wr2_sb = load_blocks("wr2_sb", wr2)
 
-        identity = held.tile([P, P], F32, name="identity")
+        identity = held.tile([BIAS_ROWS, BIAS_ROWS], F32, name="identity")
         make_identity(nc, identity[:])
-        flipped = banks[BANKS - 1][:, 0:P]
+        flipped = banks[BANKS - 1][:, 0:BIAS_ROWS]
         nc.tensor.transpose(flipped, bias_rows[:], identity[:])
-        bias_cols = held.tile([P, P], F32, name="bias_cols")
+        bias_cols = held.tile([P, BIAS_ROWS], F32, name="bias_cols")
         nc.vector.tensor_copy(bias_cols[:], flipped)
 
         def bias(name, block):
@@ -192,10 +193,19 @@ def tile_efficientrelationshipmodel_b_kernel(
             for d in range(DO // P):
                 staged = staging.tile([P, STORE], F32, name="staged")
                 for c in range(STORE // E):
-                    acc = project(nc, next_bank(), wr2_sb, 0, hid_banks[c], d, 0, E)
-                    add_bias(
-                        nc, vector_helps and c < 2, staged[:, c * E : (c + 1) * E], acc, bias("br2", d), relu=False
-                    )
+                    very_last = window == len(group_of) - 1 and d == DO // P - 1 and c == STORE // E - 1
+                    for part in range(2 if very_last else 1):
+                        width = E // 2 if very_last else E
+                        at = part * width
+                        acc = project(nc, next_bank(), wr2_sb, 0, hid_banks[c], d, at, width)
+                        add_bias(
+                            nc,
+                            part == 0 if very_last else vector_helps and c < 2,
+                            staged[:, c * E + at : c * E + at + width],
+                            acc,
+                            bias("br2", d),
+                            relu=False,
+                        )
                 nc.sync.dma_start(out[d * P : (d + 1) * P, window * STORE : (window + 1) * STORE], staged[:])
 
         for piece in pieces_of(0):

import concourse.mybir as mybir
from concourse.masks import make_identity

BF16 = mybir.dt.bfloat16
F32 = mybir.dt.float32
U16 = mybir.dt.uint16
ADD = mybir.AluOpType.add
MAX = mybir.AluOpType.max
RELU = mybir.ActivationFunctionType.Relu
IDENTITY = mybir.ActivationFunctionType.Identity

P = 128
S = 4096
E = 512
H = 512
EO = 1024
R = 256
DO = 256
B = 8
NE = 64
GROUPS = (4, 4)
BIAS_ROWS = 64
STORE = 2048
BANKS = 8
AHEAD = 3
HELPED = 2

FLOPS = 2 * (P * H * 2 * E + 2 * H * H * E + EO * EO * E + 2 * EO * R * E + R * DO * B * NE * NE)


def add_bias(nc, on_vector, dest, acc, bias_col, relu):
    if not on_vector:
        nc.scalar.activation(dest, acc, RELU if relu else IDENTITY, bias=bias_col)
    elif relu:
        nc.vector.tensor_scalar(dest, acc, bias_col, 0.0, ADD, MAX)
    else:
        nc.vector.tensor_scalar_add(dest, acc, bias_col)


def project(nc, bank, weights, first_k, moving, m, at, width):
    acc = bank[:, 0:width]
    last = len(moving) - 1
    for k, block in enumerate(moving):
        nc.tensor.matmul(
            acc,
            weights[:, first_k + k, m * P : (m + 1) * P],
            block[:, at : at + width],
            start=(k == 0),
            stop=(k == last),
        )
    return acc


def tile_efficientrelationshipmodel_b_kernel(
    tc, table, ws1, bs1, ws2, bs2, we1, be1, we2, be2, wo, bo, wr1, br1, wr2, br2, offs, out
):
    nc = tc.nc
    with (
        tc.tile_pool(name="held", bufs=1) as held,
        tc.tile_pool(name="pairs", bufs=(AHEAD + 1) * (STORE // E)) as pairs,
        tc.tile_pool(name="staging", bufs=6) as staging,
        tc.psum_pool(name="psum", bufs=1) as psum,
    ):
        banks = [psum.tile([P, E], F32, name=f"bank{b}") for b in range(BANKS)]
        taken = []

        def next_bank():
            taken.append(len(taken))
            return banks[taken[-1] % BANKS]

        def load_blocks(name, weights):
            rows, columns = weights.shape
            tile = held.tile([P, rows // P, columns], BF16, name=name)
            nc.sync.dma_start(tile[:], weights.rearrange("(k p) c -> p k c", p=P))
            return tile

        offsets = held.tile([P, 2 * E // 16], U16, name="offsets")
        nc.sync.dma_start(offsets[:], offs)
        ws1_sb = load_blocks("ws1_sb", ws1)
        table_sb = held.tile([P, S], BF16, name="table_sb")
        nc.sync.dma_start(table_sb[:], table)

        bias_rows = held.tile([BIAS_ROWS, P], F32, name="bias_rows")
        nc.gpsimd.memset(bias_rows[:], 0.0)
        first_col = {}
        rows_used = 0
        for name, vector in (
            ("bs1", bs1), ("be1", be1), ("bs2", bs2), ("be2", be2), ("bo", bo), ("br1", br1), ("br2", br2)
        ):
            blocks = vector.shape[0] // P
            nc.sync.dma_start(
                bias_rows[rows_used : rows_used + blocks, :], vector.rearrange("(k p) o -> k (p o)", p=P)
            )
            first_col[name] = rows_used
            rows_used += blocks

        we1_sb = load_blocks("we1_sb", we1)
        ws2_sb = load_blocks("ws2_sb", ws2)
        we2_sb = load_blocks("we2_sb", we2)
        wo_sb = load_blocks("wo_sb", wo)
        wr1_sb = load_blocks("wr1_sb", wr1)
        wr2_sb = load_blocks("wr2_sb", wr2)

        identity = held.tile([BIAS_ROWS, BIAS_ROWS], F32, name="identity")
        make_identity(nc, identity[:])
        flipped = banks[BANKS - 1][:, 0:BIAS_ROWS]
        nc.tensor.transpose(flipped, bias_rows[:], identity[:])
        bias_cols = held.tile([P, BIAS_ROWS], F32, name="bias_cols")
        nc.vector.tensor_copy(bias_cols[:], flipped)

        def bias(name, block):
            col = first_col[name] + block
            return bias_cols[:, col : col + 1]

        a = []
        for side, (w1_sb, b1) in enumerate(((ws1_sb, "bs1"), (we1_sb, "be1"))):
            picked = table_sb[:].indirect(offsets[:, side * (E // 16) : (side + 1) * (E // 16)])
            a.append([])
            for m in range(H // P):
                bank = next_bank()
                nc.tensor.matmul(bank[:], w1_sb[:, 0, m * P : (m + 1) * P], picked, start=True, stop=True)
                a_block = held.tile([P, E], BF16, name=f"a{side}_{m}")
                add_bias(nc, m % 2 == 1, a_block[:], bank[:], bias(b1, m), relu=True)
                a[side].append(a_block)

        widths = [batches * NE for batches in GROUPS]
        starts = [sum(widths[:g]) for g in range(len(GROUPS))]
        cat = [[] for g in GROUPS]
        ent = [[] for g in GROUPS]
        hp = [[] for g in GROUPS]
        hq = [[] for g in GROUPS]

        def odd_on_vector(g, m):
            return g == 0 and m % 2 == 1

        def stage2(g, side):
            w2_sb, b2 = ((ws2_sb, "bs2"), (we2_sb, "be2"))[side]
            for m in range(H // P):
                acc = project(nc, next_bank(), w2_sb, 0, a[side], m, starts[g], widths[g])
                cat_block = held.tile([P, widths[g]], BF16, name=f"cat{g}_{side}_{m}")
                add_bias(nc, odd_on_vector(g, m), cat_block[:], acc, bias(b2, m), relu=True)
                cat[g].append(cat_block)

        def stage3(g, blocks):
            for m in blocks:
                acc = project(nc, next_bank(), wo_sb, 0, cat[g], m, 0, widths[g])
                ent_block = held.tile([P, widths[g]], BF16, name=f"ent{g}_{m}")
                add_bias(nc, odd_on_vector(g, m), ent_block[:], acc, bias("bo", m), relu=False)
                ent[g].append(ent_block)

        def stage4(g, m):
            hp_block = held.tile([P, widths[g]], F32, name=f"hp{g}_{m}")
            acc = project(nc, next_bank(), wr1_sb, 0, ent[g], m, 0, widths[g])
            nc.scalar.activation(hp_block[:], acc, IDENTITY, bias=bias("br1", m))
            hp[g].append(hp_block)
            hq_block = held.tile([P, widths[g]], F32, name=f"hq{g}_{m}")
            acc = project(nc, next_bank(), wr1_sb, EO // P, ent[g], m, 0, widths[g])
            if g == 0:
                nc.vector.tensor_copy(hq_block[:], acc)
            else:
                nc.scalar.copy(hq_block[:], acc)
            hq[g].append(hq_block)

        def pieces_of(g):
            calls = [lambda side=side: stage2(g, side) for side in range(2)]
            calls += [lambda m=m: stage3(g, (m, m + 1)) for m in range(0, EO // P, 2)]
            calls += [lambda m=m: stage4(g, m) for m in range(R // P)]
            return calls

        group_of = [g for g, batches in enumerate(GROUPS) for w in range(batches * NE * NE // STORE)]

        def make_hid(window):
            g = group_of[window]
            hid_banks = []
            for c in range(STORE // E):
                hid = [pairs.tile([P, E], BF16, name=f"hid{m}") for m in range(R // P)]
                for i in range(E // NE):
                    p = window * (STORE // NE) + c * (E // NE) + i - starts[g]
                    batch = p // NE
                    for m in range(R // P):
                        nc.vector.tensor_scalar(
                            hid[m][:, i * NE : (i + 1) * NE],
                            hq[g][m][:, batch * NE : (batch + 1) * NE],
                            hp[g][m][:, p : p + 1],
                            0.0,
                            ADD,
                            MAX,
                        )
                hid_banks.append(hid)
            return hid_banks

        def make_out(window, hid_banks, vector_helps):
            for d in range(DO // P):
                staged = staging.tile([P, STORE], F32, name="staged")
                for c in range(STORE // E):
                    very_last = window == len(group_of) - 1 and d == DO // P - 1 and c == STORE // E - 1
                    for part in range(2 if very_last else 1):
                        width = E // 2 if very_last else E
                        at = part * width
                        acc = project(nc, next_bank(), wr2_sb, 0, hid_banks[c], d, at, width)
                        add_bias(
                            nc,
                            part == 0 if very_last else vector_helps and c < 2,
                            staged[:, c * E + at : c * E + at + width],
                            acc,
                            bias("br2", d),
                            relu=False,
                        )
                nc.sync.dma_start(out[d * P : (d + 1) * P, window * STORE : (window + 1) * STORE], staged[:])

        for piece in pieces_of(0):
            piece()

        before = {}
        for g in range(1, len(GROUPS)):
            pieces = pieces_of(g)
            own = [window for window, owner in enumerate(group_of) if owner == g - 1]
            before[own[0]] = pieces[:2]
            for i, piece in enumerate(pieces[2:]):
                before.setdefault(own[1 + i * (len(own) - 2) // len(pieces[2:])], []).append(piece)

        windows = len(group_of)
        hid_of = []
        for window in range(windows):
            for piece in before.get(window, []):
                piece()
            while len(hid_of) < min(window + 1 + AHEAD, windows) and len(hq[group_of[len(hid_of)]]) == R // P:
                hid_of.append(make_hid(len(hid_of)))
            make_out(window, hid_of[window], vector_helps=(window + HELPED >= windows))
